import numpy as np
import ml_dtypes


def mxq(x, axis, fmt="e4m3"):
    dtype, down = {"e4m3": (ml_dtypes.float8_e4m3fn, 7), "e5m2": (ml_dtypes.float8_e5m2, 14)}[fmt]
    v = np.moveaxis(np.asarray(x, np.float32).astype(ml_dtypes.bfloat16).astype(np.float64), axis, -1)
    blocks = v.reshape(v.shape[:-1] + (-1, 32))
    amax = np.abs(blocks).max(-1, keepdims=True)
    byte = np.maximum(np.where(amax > 0, np.frexp(amax)[1] - 1 + 127, 0) - down, 1)
    scale = np.exp2(byte - 127.0)
    codes = (blocks / scale).astype(np.float32).astype(dtype).astype(np.float64)
    return np.moveaxis((codes * scale).reshape(v.shape), -1, axis)


WIDE = False


def mx_kscale(k):
    if not WIDE:
        return np.ones(k)
    levels = np.array([10, -10, 5, -5, 0])
    a = np.random.permutation(np.resize(levels, k // 512 * 4)).reshape(k // 512, 4)
    idx = np.arange(k)
    return np.exp2(a[idx // 512, idx % 128 // 32])


BF16 = ml_dtypes.bfloat16


def bf(x):
    return np.asarray(x, np.float32).astype(BF16)


def f64(x):
    return np.asarray(x).astype(np.float64)


E2M1 = np.array([0.0, 0.5, 1.0, 1.5, 2.0, 3.0, 4.0, 6.0, -0.0, -0.5, -1.0, -1.5, -2.0, -3.0, -4.0, -6.0])


def pack_weight(w, fmt):
    k, n = w.shape
    w = f64(bf(w)).reshape(k // 32, 32, n)
    amax = np.abs(w).max(1)
    if fmt == "e4m3":
        byte = np.frexp(amax)[1] - 1 + 127 - 7
    else:
        mant, ex = np.frexp(amax / 6.0)
        byte = np.where(mant > 0.5, ex, ex - 1) + 127
    byte = np.clip(np.where(amax > 0, byte, 1), 1, 254)
    scaled = (w * np.exp2(127.0 - byte)[:, None, :]).reshape(k, n).astype(np.float32)
    by_word = np.ascontiguousarray(scaled.reshape(k // 512, 128, 4, n).transpose(0, 1, 3, 2))
    if fmt == "e4m3":
        words = by_word.astype(ml_dtypes.float8_e4m3fn).view(np.uint8)
    else:
        c = by_word.astype(ml_dtypes.float4_e2m1fn).view(np.uint8) & 0xF
        words = c[..., 0::2] | (c[..., 1::2] << 4)
    return np.ascontiguousarray(words), np.ascontiguousarray(byte.astype(np.uint8).reshape(k // 512, 16, n))


def unpack_weight(words, scales, fmt):
    g, p, n, _ = words.shape
    if fmt == "e4m3":
        vals = np.ascontiguousarray(words).view(ml_dtypes.float8_e4m3fn).astype(np.float64)
    else:
        nib = np.empty((g, p, n, 4), np.uint8)
        nib[..., 0::2] = words & 0xF
        nib[..., 1::2] = words >> 4
        vals = E2M1[nib]
    vals = vals * np.repeat(np.exp2(scales.astype(np.float64) - 127.0), 8, axis=1)[..., None]
    return vals.transpose(0, 1, 3, 2).reshape(g * 512, n)


B, S, D, H, NOPE, ROPE, VD, KV_RANK, Q_RANK = 2, 64, 1024, 16, 128, 64, 128, 512, 8192
EPS = 1e-6
THETA = 10000.0
LAT = 0.005
HALF = ROPE // 2
QK = NOPE + ROPE
FMT = "e4m3"


def rmsnorm(v, g):
    return v * (1.0 / np.sqrt(np.mean(v * v, axis=-1, keepdims=True) + EPS)) * g


def rope(v):
    inv = 1.0 / THETA ** (np.arange(HALF) / HALF)
    ang = np.arange(S)[:, None] * inv[None, :]
    cos = np.cos(ang)[None, :, None, :]
    sin = np.sin(ang)[None, :, None, :]
    v1, v2 = v[..., :HALF], v[..., HALF:]
    return np.concatenate([v1 * cos - v2 * sin, v2 * cos + v1 * sin], axis=-1)


def setup_inputs():
    s, t = mx_kscale(D), mx_kscale(Q_RANK)
    x = bf(np.random.standard_normal((B, S, D)) * s)
    w_dq_words, w_dq_scales = pack_weight(np.random.standard_normal((D, Q_RANK)) * LAT / np.sqrt(D) / s[:, None], FMT)
    q_a_norm = bf((1.0 + 0.1 * np.random.standard_normal(Q_RANK)) * t)
    w_uq_words, w_uq_scales = pack_weight(np.random.standard_normal((Q_RANK, H * QK)) / np.sqrt(Q_RANK) / t[:, None], FMT)
    return {"x": x,
            "w_dq_words": w_dq_words,
            "w_dq_scales": w_dq_scales,
            "q_a_norm": q_a_norm,
            "w_uq_words": w_uq_words,
            "w_uq_scales": w_uq_scales}


def reference(x, w_dq_words, w_dq_scales, q_a_norm, w_uq_words, w_uq_scales):
    c_q = mxq(f64(x), 2, "e4m3") @ unpack_weight(w_dq_words, w_dq_scales, FMT)
    h = rmsnorm(c_q, f64(q_a_norm))
    q = (mxq(h, 2, "e4m3") @ unpack_weight(w_uq_words, w_uq_scales, FMT)).reshape(B, S, H, QK)
    q_nope, q_pe = q[..., :NOPE], q[..., NOPE:]
    return np.concatenate([q_nope, rope(q_pe)], axis=-1)

@@ -1,0 +1,297 @@
+import math
+from contextlib import ExitStack
+
+import concourse.mybir as mybir
+from concourse.masks import make_identity
+
+F32 = mybir.dt.float32
+BF16 = mybir.dt.bfloat16
+I32 = mybir.dt.int32
+U32 = mybir.dt.uint32
+U8 = mybir.dt.uint8
+FP8X4 = mybir.dt.float8_e4m3fn_x4
+ALU = mybir.AluOpType
+ACT = mybir.ActivationFunctionType
+
+B, S, D, H, NOPE, ROPE, Q_RANK = 2, 64, 1024, 16, 128, 64, 8192
+HALF = ROPE // 2
+DOUBLINGS = 5
+assert 2**DOUBLINGS == HALF
+QK = NOPE + ROPE
+N_OUT = H * QK
+EPS = 1e-6
+THETA = 10000.0
+
+P = 128
+K_PASS = 512
+BANK = 512
+DQ_PASSES = D // K_PASS
+UQ_PASSES = Q_RANK // K_PASS
+PLANES = 4
+DQ_BLOCK = Q_RANK // PLANES
+H_CHUNK = 4 * K_PASS
+TAIL_PASSES = 2
+TAIL_BLOCK = 2 * BANK
+
+FLOPS = 2 * P * (D * Q_RANK + Q_RANK * N_OUT)
+
+
+def quantise_tokens(nc, psum, work, ident, rows, codes, planes):
+    words = rows.bitcast(F32)
+    groups = words.shape[1] // (K_PASS // 2)
+    grouped = work.tile([P, groups * K_PASS], BF16, align_bytes=64, tag="grouped")
+    grouped_words = grouped[:].bitcast(F32).rearrange("p (g r u) -> p g r u", r=P, u=2)
+    for pair in range(groups // 2):
+        flipped = psum.tile([P, 2, 2, P], F32, tag="bank")
+        for j in range(2):
+            first = (2 * pair + j) * (K_PASS // 2)
+            for u in range(2):
+                nc.tensor.transpose(
+                    flipped[:, j, u, :], words[:, first + u : first + K_PASS // 2 : 2], ident[:]
+                )
+        nc.scalar.copy(
+            out=grouped_words[:, 2 * pair : 2 * pair + 2, :, :],
+            in_=flipped[:].rearrange("p g u r -> p g r u"),
+        )
+    nc.vector.quantize_mx(out=codes.bitcast(FP8X4), scales=planes, in_=grouped[:])
+
+
+def tile_multiheadlatentattention_pa_k_kernel(
+    tc, x, w_dq_words, w_dq_scales, q_a_norm, w_uq_words, w_uq_scales, out
+):
+    nc = tc.nc
+    out_flat = out.rearrange("b s h f -> (b s) (h f)")
+    with ExitStack() as stack:
+        keep = stack.enter_context(tc.tile_pool(name="keep", bufs=1))
+        work = stack.enter_context(tc.tile_pool(name="work", bufs=2))
+        block_pool = stack.enter_context(tc.tile_pool(name="block_words", bufs=4))
+        pass_pool = stack.enter_context(tc.tile_pool(name="pass_words", bufs=6))
+        psum = stack.enter_context(tc.psum_pool(name="psum", bufs=8))
+
+        dq_planes = keep.tile([P, DQ_PASSES, DQ_BLOCK], U8, align_bytes=64)
+        uq_planes = keep.tile([P, UQ_PASSES // PLANES, N_OUT], U8, align_bytes=64)
+        nc.vector.memset(dq_planes[:].bitcast(I32), 0)
+        nc.vector.memset(uq_planes[:].bitcast(I32), 0)
+        for g in range(DQ_PASSES):
+            for quad in range(4):
+                nc.sync.dma_start(
+                    out=dq_planes[32 * quad : 32 * quad + 16, g, :].bitcast(I32),
+                    in_=w_dq_scales[g, 4 * quad : 4 * quad + 4, :]
+                    .bitcast(I32)
+                    .rearrange("r (j n) -> j r n", j=PLANES),
+                )
+        for a in range(UQ_PASSES // PLANES):
+            for quad in range(4):
+                nc.sync.dma_start(
+                    out=uq_planes[32 * quad : 32 * quad + 16, a, :].bitcast(I32),
+                    in_=w_uq_scales[
+                        PLANES * a : PLANES * (a + 1), 4 * quad : 4 * quad + 4, :
+                    ].bitcast(I32),
+                )
+
+        x_rows = keep.tile([P, D], BF16)
+        nc.scalar.dma_start(out=x_rows[:], in_=x.flatten_outer_dims())
+        gain_rows = keep.tile([P, BANK], BF16)
+        nc.vector.memset(gain_rows[:], 0.0)
+        nc.scalar.dma_start(
+            out=gain_rows[0 : Q_RANK // BANK, :], in_=q_a_norm.rearrange("(c n) -> c n", n=BANK)
+        )
+
+        ident = keep.tile([P, P], F32)
+        make_identity(nc, ident[:])
+        ident_bf = keep.tile([P, P], BF16)
+        make_identity(nc, ident_bf[:])
+
+        x_codes = keep.tile([P, DQ_PASSES * P], U32, align_bytes=64)
+        x_planes = keep.tile([P, DQ_PASSES * P], U8, align_bytes=64)
+        quantise_tokens(nc, psum, work, ident, x_rows[:], x_codes[:], x_planes[:])
+
+        gain_all = keep.tile([P, Q_RANK], BF16)
+        for c in range(Q_RANK // BANK):
+            spread = psum.tile([P, BANK], F32, tag="bank")
+            nc.tensor.matmul(
+                out=spread[:],
+                lhsT=ident_bf[:, c : c + 1].to_broadcast([P, P]),
+                rhs=gain_rows[:],
+                start=True,
+                stop=True,
+            )
+            if c % 2 == 0:
+                nc.scalar.copy(out=gain_all[:, c * BANK : (c + 1) * BANK], in_=spread[:])
+            else:
+                nc.vector.tensor_copy(out=gain_all[:, c * BANK : (c + 1) * BANK], in_=spread[:])
+
+        pos_int = keep.tile([P, 1], I32)
+        for b in range(B):
+            nc.gpsimd.iota(pos_int[b * S : (b + 1) * S, :], pattern=[[0, 1]], base=0, channel_multiplier=1)
+        pos = keep.tile([P, 1], F32)
+        nc.vector.tensor_copy(out=pos[:], in_=pos_int[:])
+        base_turns = keep.tile([P, HALF], F32)
+        nc.vector.tensor_scalar(
+            out=base_turns[:, 0:1], in0=pos[:], scalar1=1.0 / (2.0 * math.pi), scalar2=None, op0=ALU.mult
+        )
+        for doubling in range(DOUBLINGS):
+            width = 2**doubling
+            nc.vector.tensor_scalar(
+                out=base_turns[:, width : 2 * width],
+                in0=base_turns[:, 0:width],
+                scalar1=THETA ** (-width / HALF),
+                scalar2=None,
+                op0=ALU.mult,
+            )
+        turns = keep.tile([P, 2, 2, HALF], F32)
+        for k, phase in enumerate((0.25, 0.0)):
+            nc.vector.tensor_scalar(
+                out=turns[:, k, :, :],
+                in0=base_turns[:].unsqueeze(1).to_broadcast([P, 2, HALF]),
+                scalar1=phase,
+                scalar2=None,
+                op0=ALU.add,
+            )
+        whole_int = keep.tile([P, 2, 2, HALF], I32)
+        nc.vector.tensor_copy(out=whole_int[:], in_=turns[:])
+        whole = keep.tile([P, 2, 2, HALF], F32)
+        nc.vector.tensor_copy(out=whole[:], in_=whole_int[:])
+        part = keep.tile([P, 2 * ROPE], F32)
+        nc.vector.tensor_tensor(
+            out=part[:],
+            in0=turns[:].rearrange("p k j i -> p (k j i)"),
+            in1=whole[:].rearrange("p k j i -> p (k j i)"),
+            op=ALU.subtract,
+        )
+        minus_part = keep.tile([P, 2 * ROPE], F32)
+        nc.vector.scalar_tensor_tensor(
+            out=minus_part[:], in0=part[:], scalar=0.5, in1=part[:], op0=ALU.is_gt, op1=ALU.subtract
+        )
+        cos_sin = keep.tile([P, 2, ROPE], F32)
+        nc.scalar.activation(
+            out=cos_sin[:].rearrange("p k f -> p (k f)"),
+            in_=minus_part[:],
+            func=ACT.Sin,
+            scale=-2.0 * math.pi,
+        )
+
+        c_gain = keep.tile([P, Q_RANK], F32)
+        square_sums = keep.tile([P, Q_RANK // BANK], F32)
+        for blk in range(PLANES):
+            banks = [psum.tile([P, BANK], F32, tag="bank", name="c_bank%d" % i) for i in range(4)]
+            for g in range(DQ_PASSES):
+                w_block = block_pool.tile([P, DQ_BLOCK], I32, align_bytes=64, tag="w_block")
+                nc.sync.dma_start(
+                    out=w_block[:],
+                    in_=w_dq_words[g]
+                    .rearrange("p n t -> p (n t)")[:, 4 * DQ_BLOCK * blk : 4 * DQ_BLOCK * (blk + 1)]
+                    .bitcast(I32),
+                )
+                for i in range(4):
+                    nc.tensor.matmul_mx(
+                        out=banks[i][:],
+                        lhsT=x_codes[:, g * P : (g + 1) * P].bitcast(FP8X4),
+                        lhsT_scale=x_planes[:, g * P : (g + 1) * P],
+                        rhs=w_block[:, i * BANK : (i + 1) * BANK].bitcast(FP8X4),
+                        rhs_scale=dq_planes[4 * blk : P, g, i * BANK : (i + 1) * BANK],
+                        start=(g == 0),
+                        stop=(g == DQ_PASSES - 1),
+                    )
+            for i in range(4):
+                c = 4 * blk + i
+                cols = slice(c * BANK, (c + 1) * BANK)
+                nc.scalar.activation(
+                    out=c_gain[:, cols], in_=banks[i][:], func=ACT.Square, accum_out=square_sums[:, c : c + 1]
+                )
+                nc.vector.tensor_tensor(out=c_gain[:, cols], in0=banks[i][:], in1=gain_all[:, cols], op=ALU.mult)
+
+        square_sum = keep.tile([P, 1], F32)
+        nc.vector.reduce_sum(out=square_sum[:], in_=square_sums[:], axis=mybir.AxisListType.X)
+        rms = keep.tile([P, 1], F32)
+        nc.scalar.activation(out=rms[:], in_=square_sum[:], func=ACT.Sqrt, bias=EPS, scale=1.0 / Q_RANK)
+        inv_rms = keep.tile([P, 1], F32)
+        nc.vector.reciprocal(out=inv_rms[:], in_=rms[:])
+
+        h_codes = keep.tile([P, UQ_PASSES * P], U32, align_bytes=64)
+        h_planes = keep.tile([P, UQ_PASSES * P], U8, align_bytes=64)
+        for chunk in range(Q_RANK // H_CHUNK):
+            h_rows = work.tile([P, H_CHUNK], BF16, tag="h_rows")
+            nc.vector.tensor_scalar(
+                out=h_rows[:],
+                in0=c_gain[:, chunk * H_CHUNK : (chunk + 1) * H_CHUNK],
+                scalar1=inv_rms[:, 0:1],
+                scalar2=None,
+                op0=ALU.mult,
+            )
+            cols = slice(chunk * H_CHUNK // 4, (chunk + 1) * H_CHUNK // 4)
+            quantise_tokens(nc, psum, work, ident, h_rows[:], h_codes[:, cols], h_planes[:, cols])
+
+        q_banks = [psum.tile([P, BANK], F32, tag="bank", name="q_bank%d" % i) for i in range(N_OUT // BANK)]
+
+        def uq_pass(g, bank, words):
+            nc.tensor.matmul_mx(
+                out=q_banks[bank][:],
+                lhsT=h_codes[:, g * P : (g + 1) * P].bitcast(FP8X4),
+                lhsT_scale=h_planes[:, g * P : (g + 1) * P],
+                rhs=words.bitcast(FP8X4),
+                rhs_scale=uq_planes[4 * (g % PLANES) : P, g // PLANES, bank * BANK : (bank + 1) * BANK],
+                start=(g == 0),
+                stop=(g == UQ_PASSES - 1),
+            )
+
+        for g in range(UQ_PASSES - TAIL_PASSES):
+            w_pass = pass_pool.tile([P, N_OUT], I32, align_bytes=64, tag="w_pass")
+            nc.sync.dma_start(out=w_pass[:], in_=w_uq_words[g].rearrange("p n t -> p (n t)").bitcast(I32))
+            for bank in range(N_OUT // BANK):
+                uq_pass(g, bank, w_pass[:, bank * BANK : (bank + 1) * BANK])
+
+        w_tails = []
+        for blk in range(N_OUT // TAIL_BLOCK):
+            first_col = blk * TAIL_BLOCK
+            w_tail = block_pool.tile([P, TAIL_PASSES, TAIL_BLOCK], I32, align_bytes=64, tag="w_block")
+            nc.sync.dma_start(
+                out=w_tail[:],
+                in_=w_uq_words[UQ_PASSES - TAIL_PASSES : UQ_PASSES, :, first_col : first_col + TAIL_BLOCK, :]
+                .rearrange("g p n t -> p g (n t)")
+                .bitcast(I32),
+            )
+            w_tails.append(w_tail)
+        q_rows = keep.tile([P, N_OUT + NOPE], F32)
+        for blk in range(N_OUT // TAIL_BLOCK):
+            first_col = blk * TAIL_BLOCK
+            w_tail = w_tails[blk]
+            for j in range(TAIL_PASSES):
+                for i in range(TAIL_BLOCK // BANK):
+                    uq_pass(
+                        UQ_PASSES - TAIL_PASSES + j,
+                        first_col // BANK + i,
+                        w_tail[:, j, i * BANK : (i + 1) * BANK],
+                    )
+            nc.scalar.copy(out=q_rows[:, first_col : first_col + BANK], in_=q_banks[first_col // BANK][:])
+            nc.vector.tensor_copy(
+                out=q_rows[:, first_col + BANK : first_col + 2 * BANK], in_=q_banks[first_col // BANK + 1][:]
+            )
+            heads = [h for h in range(H) if first_col <= h * QK + NOPE < first_col + TAIL_BLOCK]
+            n_heads = len(heads)
+            rotated = q_rows[:, heads[0] * QK + NOPE : (heads[0] + n_heads) * QK + NOPE].rearrange(
+                "p (h f) -> p h f", f=QK
+            )[:, :, 0:ROPE]
+            products = work.tile([P, n_heads, 2, ROPE], F32, tag="products")
+            nc.vector.tensor_tensor(
+                out=products[:],
+                in0=rotated.unsqueeze(2).to_broadcast([P, n_heads, 2, ROPE]),
+                in1=cos_sin[:].unsqueeze(1).to_broadcast([P, n_heads, 2, ROPE]),
+                op=ALU.mult,
+            )
+            nc.vector.tensor_tensor(
+                out=rotated[:, :, 0:HALF],
+                in0=products[:, :, 0, 0:HALF],
+                in1=products[:, :, 1, HALF:ROPE],
+                op=ALU.subtract,
+            )
+            nc.vector.tensor_tensor(
+                out=rotated[:, :, HALF:ROPE],
+                in0=products[:, :, 0, HALF:ROPE],
+                in1=products[:, :, 1, 0:HALF],
+                op=ALU.add,
+            )
+            nc.sync.dma_start(
+                out=out_flat[:, first_col : first_col + TAIL_BLOCK],
+                in_=q_rows[:, first_col : first_col + TAIL_BLOCK],
+            )

@@ -82,11 +82,11 @@ def tile_multiheadlatentattention_pa_k_kernel(
                 )
         for a in range(UQ_PASSES // PLANES):
             for quad in range(4):
-                nc.sync.dma_start(
-                    out=uq_planes[32 * quad : 32 * quad + 16, a, :].bitcast(I32),
+                nc.gpsimd.dma_start(
+                    out=uq_planes[32 * quad : 32 * quad + 16, a, :].bitcast(F32),
                     in_=w_uq_scales[
                         PLANES * a : PLANES * (a + 1), 4 * quad : 4 * quad + 4, :
-                    ].bitcast(I32),
+                    ].bitcast(F32),
                 )
 
         x_rows = keep.tile([P, D], BF16)

@@ -30,8 +30,10 @@ UQ_PASSES = Q_RANK // K_PASS
 PLANES = 4
 DQ_BLOCK = Q_RANK // PLANES
 H_CHUNK = 4 * K_PASS
+CHUNK_PASSES = H_CHUNK // K_PASS
 TAIL_PASSES = 2
-TAIL_BLOCK = 2 * BANK
+MAIN_PASSES = UQ_PASSES - TAIL_PASSES
+TAIL_BANKS = N_OUT // BANK // TAIL_PASSES
 
 FLOPS = 2 * P * (D * Q_RANK + Q_RANK * N_OUT)
 
@@ -42,7 +44,7 @@ def quantise_tokens(nc, psum, work, ident, rows, codes, planes):
     grouped = work.tile([P, groups * K_PASS], BF16, align_bytes=64, tag="grouped")
     grouped_words = grouped[:].bitcast(F32).rearrange("p (g r u) -> p g r u", r=P, u=2)
     for pair in range(groups // 2):
-        flipped = psum.tile([P, 2, 2, P], F32, tag="bank")
+        flipped = psum.tile([P, 2, 2, P], F32, tag="short", bufs=2)
         for j in range(2):
             first = (2 * pair + j) * (K_PASS // 2)
             for u in range(2):
@@ -65,8 +67,8 @@ def tile_multiheadlatentattention_pa_k_kernel(
         keep = stack.enter_context(tc.tile_pool(name="keep", bufs=1))
         work = stack.enter_context(tc.tile_pool(name="work", bufs=2))
         block_pool = stack.enter_context(tc.tile_pool(name="block_words", bufs=4))
-        pass_pool = stack.enter_context(tc.tile_pool(name="pass_words", bufs=6))
-        psum = stack.enter_context(tc.psum_pool(name="psum", bufs=8))
+        pass_pool = stack.enter_context(tc.tile_pool(name="pass_words", bufs=7))
+        psum = stack.enter_context(tc.psum_pool(name="psum", bufs=6))
 
         dq_planes = keep.tile([P, DQ_PASSES, DQ_BLOCK], U8, align_bytes=64)
         uq_planes = keep.tile([P, UQ_PASSES // PLANES, N_OUT], U8, align_bytes=64)
@@ -82,11 +84,11 @@ def tile_multiheadlatentattention_pa_k_kernel(
                 )
         for a in range(UQ_PASSES // PLANES):
             for quad in range(4):
-                nc.gpsimd.dma_start(
-                    out=uq_planes[32 * quad : 32 * quad + 16, a, :].bitcast(F32),
+                nc.sync.dma_start(
+                    out=uq_planes[32 * quad : 32 * quad + 16, a, :].bitcast(I32),
                     in_=w_uq_scales[
                         PLANES * a : PLANES * (a + 1), 4 * quad : 4 * quad + 4, :
-                    ].bitcast(F32),
+                    ].bitcast(I32),
                 )
 
         x_rows = keep.tile([P, D], BF16)
@@ -108,7 +110,7 @@ def tile_multiheadlatentattention_pa_k_kernel(
 
         gain_all = keep.tile([P, Q_RANK], BF16)
         for c in range(Q_RANK // BANK):
-            spread = psum.tile([P, BANK], F32, tag="bank")
+            spread = psum.tile([P, BANK], F32, tag="short", bufs=2)
             nc.tensor.matmul(
                 out=spread[:],
                 lhsT=ident_bf[:, c : c + 1].to_broadcast([P, P]),
@@ -170,11 +172,13 @@ def tile_multiheadlatentattention_pa_k_kernel(
             func=ACT.Sin,
             scale=-2.0 * math.pi,
         )
+        warm = keep.tile([P, 1], F32)
+        nc.scalar.activation(out=warm[:], in_=cos_sin[:, 0, 0:1], func=ACT.Sqrt, bias=1.0, scale=0.0)
 
-        c_gain = keep.tile([P, Q_RANK], F32)
+        c_gain = keep.tile([P, Q_RANK], F32, tag="c_gain")
         square_sums = keep.tile([P, Q_RANK // BANK], F32)
         for blk in range(PLANES):
-            banks = [psum.tile([P, BANK], F32, tag="bank", name="c_bank%d" % i) for i in range(4)]
+            banks = [psum.tile([P, BANK], F32, tag="sums", name="c_bank%d" % i) for i in range(4)]
             for g in range(DQ_PASSES):
                 w_block = block_pool.tile([P, DQ_BLOCK], I32, align_bytes=64, tag="w_block")
                 nc.sync.dma_start(
@@ -210,19 +214,7 @@ def tile_multiheadlatentattention_pa_k_kernel(
 
         h_codes = keep.tile([P, UQ_PASSES * P], U32, align_bytes=64)
         h_planes = keep.tile([P, UQ_PASSES * P], U8, align_bytes=64)
-        for chunk in range(Q_RANK // H_CHUNK):
-            h_rows = work.tile([P, H_CHUNK], BF16, tag="h_rows")
-            nc.vector.tensor_scalar(
-                out=h_rows[:],
-                in0=c_gain[:, chunk * H_CHUNK : (chunk + 1) * H_CHUNK],
-                scalar1=inv_rms[:, 0:1],
-                scalar2=None,
-                op0=ALU.mult,
-            )
-            cols = slice(chunk * H_CHUNK // 4, (chunk + 1) * H_CHUNK // 4)
-            quantise_tokens(nc, psum, work, ident, h_rows[:], h_codes[:, cols], h_planes[:, cols])
-
-        q_banks = [psum.tile([P, BANK], F32, tag="bank", name="q_bank%d" % i) for i in range(N_OUT // BANK)]
+        q_banks = [psum.tile([P, BANK], F32, tag="sums", name="q_bank%d" % i) for i in range(N_OUT // BANK)]
 
         def uq_pass(g, bank, words):
             nc.tensor.matmul_mx(
@@ -235,39 +227,41 @@ def tile_multiheadlatentattention_pa_k_kernel(
                 stop=(g == UQ_PASSES - 1),
             )
 
-        for g in range(UQ_PASSES - TAIL_PASSES):
-            w_pass = pass_pool.tile([P, N_OUT], I32, align_bytes=64, tag="w_pass")
-            nc.sync.dma_start(out=w_pass[:], in_=w_uq_words[g].rearrange("p n t -> p (n t)").bitcast(I32))
-            for bank in range(N_OUT // BANK):
-                uq_pass(g, bank, w_pass[:, bank * BANK : (bank + 1) * BANK])
+        for chunk in range(Q_RANK // H_CHUNK):
+            h_rows = work.tile([P, H_CHUNK], BF16, tag="h_rows")
+            nc.vector.tensor_scalar(
+                out=h_rows[:],
+                in0=c_gain[:, chunk * H_CHUNK : (chunk + 1) * H_CHUNK],
+                scalar1=inv_rms[:, 0:1],
+                scalar2=None,
+                op0=ALU.mult,
+            )
+            cols = slice(chunk * H_CHUNK // 4, (chunk + 1) * H_CHUNK // 4)
+            quantise_tokens(nc, psum, work, ident, h_rows[:], h_codes[:, cols], h_planes[:, cols])
+            for g in range(chunk * CHUNK_PASSES, min((chunk + 1) * CHUNK_PASSES, MAIN_PASSES)):
+                w_pass = pass_pool.tile([P, N_OUT], I32, align_bytes=64, tag="w_pass")
+                nc.sync.dma_start(out=w_pass[:], in_=w_uq_words[g].rearrange("p n t -> p (n t)").bitcast(I32))
+                for bank in range(N_OUT // BANK):
+                    uq_pass(g, bank, w_pass[:, bank * BANK : (bank + 1) * BANK])
 
         w_tails = []
-        for blk in range(N_OUT // TAIL_BLOCK):
-            first_col = blk * TAIL_BLOCK
-            w_tail = block_pool.tile([P, TAIL_PASSES, TAIL_BLOCK], I32, align_bytes=64, tag="w_block")
+        for bank in range(N_OUT // BANK):
+            if bank % TAIL_BANKS == 0:
+                w_tail = pass_pool.tile([P, TAIL_BANKS, TAIL_PASSES, BANK], I32, align_bytes=64, tag="w_pass")
             nc.sync.dma_start(
-                out=w_tail[:],
-                in_=w_uq_words[UQ_PASSES - TAIL_PASSES : UQ_PASSES, :, first_col : first_col + TAIL_BLOCK, :]
+                out=w_tail[:, bank % TAIL_BANKS, :, :],
+                in_=w_uq_words[MAIN_PASSES:UQ_PASSES, :, bank * BANK : (bank + 1) * BANK, :]
                 .rearrange("g p n t -> p g (n t)")
                 .bitcast(I32),
             )
-            w_tails.append(w_tail)
-        q_rows = keep.tile([P, N_OUT + NOPE], F32)
-        for blk in range(N_OUT // TAIL_BLOCK):
-            first_col = blk * TAIL_BLOCK
-            w_tail = w_tails[blk]
+            w_tails.append(w_tail[:, bank % TAIL_BANKS, :, :])
+        q_rows = keep.tile([P, N_OUT + NOPE], F32, tag="c_gain")
+        for bank in range(N_OUT // BANK):
+            first_col = bank * BANK
             for j in range(TAIL_PASSES):
-                for i in range(TAIL_BLOCK // BANK):
-                    uq_pass(
-                        UQ_PASSES - TAIL_PASSES + j,
-                        first_col // BANK + i,
-                        w_tail[:, j, i * BANK : (i + 1) * BANK],
-                    )
-            nc.scalar.copy(out=q_rows[:, first_col : first_col + BANK], in_=q_banks[first_col // BANK][:])
-            nc.vector.tensor_copy(
-                out=q_rows[:, first_col + BANK : first_col + 2 * BANK], in_=q_banks[first_col // BANK + 1][:]
-            )
-            heads = [h for h in range(H) if first_col <= h * QK + NOPE < first_col + TAIL_BLOCK]
+                uq_pass(MAIN_PASSES + j, bank, w_tails[bank][:, j, :])
+            nc.scalar.copy(out=q_rows[:, first_col : first_col + BANK], in_=q_banks[bank][:])
+            heads = [h for h in range(H) if first_col <= h * QK + NOPE < first_col + BANK]
             n_heads = len(heads)
             rotated = q_rows[:, heads[0] * QK + NOPE : (heads[0] + n_heads) * QK + NOPE].rearrange(
                 "p (h f) -> p h f", f=QK
@@ -292,6 +286,5 @@ def tile_multiheadlatentattention_pa_k_kernel(
                 op=ALU.add,
             )
             nc.sync.dma_start(
-                out=out_flat[:, first_col : first_col + TAIL_BLOCK],
-                in_=q_rows[:, first_col : first_col + TAIL_BLOCK],
+                out=out_flat[:, first_col : first_col + BANK], in_=q_rows[:, first_col : first_col + BANK]
             )

@@ -29,7 +29,7 @@ DQ_PASSES = D // K_PASS
 UQ_PASSES = Q_RANK // K_PASS
 PLANES = 4
 DQ_BLOCK = Q_RANK // PLANES
-H_CHUNK = 4 * K_PASS
+H_CHUNK = 2 * K_PASS
 CHUNK_PASSES = H_CHUNK // K_PASS
 TAIL_PASSES = 2
 MAIN_PASSES = UQ_PASSES - TAIL_PASSES
@@ -66,22 +66,43 @@ def tile_multiheadlatentattention_pa_k_kernel(
     with ExitStack() as stack:
         keep = stack.enter_context(tc.tile_pool(name="keep", bufs=1))
         work = stack.enter_context(tc.tile_pool(name="work", bufs=2))
-        block_pool = stack.enter_context(tc.tile_pool(name="block_words", bufs=4))
+        block_pool = stack.enter_context(tc.tile_pool(name="block_words", bufs=8))
         pass_pool = stack.enter_context(tc.tile_pool(name="pass_words", bufs=7))
         psum = stack.enter_context(tc.psum_pool(name="psum", bufs=6))
+
+        x_rows = keep.tile([P, D], BF16)
+        nc.sync.dma_start(out=x_rows[:], in_=x.flatten_outer_dims())
+        gain_rows = keep.tile([P, BANK], BF16)
 
         dq_planes = keep.tile([P, DQ_PASSES, DQ_BLOCK], U8, align_bytes=64)
         uq_planes = keep.tile([P, UQ_PASSES // PLANES, N_OUT], U8, align_bytes=64)
         nc.vector.memset(dq_planes[:].bitcast(I32), 0)
+        nc.vector.memset(gain_rows[:], 0.0)
+        nc.scalar.dma_start(
+            out=gain_rows[0 : Q_RANK // BANK, :], in_=q_a_norm.rearrange("(c n) -> c n", n=BANK)
+        )
         nc.vector.memset(uq_planes[:].bitcast(I32), 0)
-        for g in range(DQ_PASSES):
-            for quad in range(4):
+
+        w_blocks = {}
+        for blk in range(PLANES):
+            for g in range(DQ_PASSES):
+                w_block = block_pool.tile([P, DQ_BLOCK], I32, align_bytes=64, tag="w_block")
                 nc.sync.dma_start(
-                    out=dq_planes[32 * quad : 32 * quad + 16, g, :].bitcast(I32),
-                    in_=w_dq_scales[g, 4 * quad : 4 * quad + 4, :]
-                    .bitcast(I32)
-                    .rearrange("r (j n) -> j r n", j=PLANES),
+                    out=w_block[:],
+                    in_=w_dq_words[g]
+                    .rearrange("p n t -> p (n t)")[:, 4 * DQ_BLOCK * blk : 4 * DQ_BLOCK * (blk + 1)]
+                    .bitcast(I32),
                 )
+                w_blocks[blk, g] = w_block
+                if blk == 0 and g == 0:
+                    for gs in range(DQ_PASSES):
+                        for quad in range(4):
+                            nc.sync.dma_start(
+                                out=dq_planes[32 * quad : 32 * quad + 16, gs, :].bitcast(I32),
+                                in_=w_dq_scales[gs, 4 * quad : 4 * quad + 4, :]
+                                .bitcast(I32)
+                                .rearrange("r (j n) -> j r n", j=PLANES),
+                            )
         for a in range(UQ_PASSES // PLANES):
             for quad in range(4):
                 nc.sync.dma_start(
@@ -91,13 +112,6 @@ def tile_multiheadlatentattention_pa_k_kernel(
                     ].bitcast(I32),
                 )
 
-        x_rows = keep.tile([P, D], BF16)
-        nc.scalar.dma_start(out=x_rows[:], in_=x.flatten_outer_dims())
-        gain_rows = keep.tile([P, BANK], BF16)
-        nc.vector.memset(gain_rows[:], 0.0)
-        nc.scalar.dma_start(
-            out=gain_rows[0 : Q_RANK // BANK, :], in_=q_a_norm.rearrange("(c n) -> c n", n=BANK)
-        )
 
         ident = keep.tile([P, P], F32)
         make_identity(nc, ident[:])
@@ -107,21 +121,6 @@ def tile_multiheadlatentattention_pa_k_kernel(
         x_codes = keep.tile([P, DQ_PASSES * P], U32, align_bytes=64)
         x_planes = keep.tile([P, DQ_PASSES * P], U8, align_bytes=64)
         quantise_tokens(nc, psum, work, ident, x_rows[:], x_codes[:], x_planes[:])
-
-        gain_all = keep.tile([P, Q_RANK], BF16)
-        for c in range(Q_RANK // BANK):
-            spread = psum.tile([P, BANK], F32, tag="short", bufs=2)
-            nc.tensor.matmul(
-                out=spread[:],
-                lhsT=ident_bf[:, c : c + 1].to_broadcast([P, P]),
-                rhs=gain_rows[:],
-                start=True,
-                stop=True,
-            )
-            if c % 2 == 0:
-                nc.scalar.copy(out=gain_all[:, c * BANK : (c + 1) * BANK], in_=spread[:])
-            else:
-                nc.vector.tensor_copy(out=gain_all[:, c * BANK : (c + 1) * BANK], in_=spread[:])
 
         pos_int = keep.tile([P, 1], I32)
         for b in range(B):
@@ -175,24 +174,17 @@ def tile_multiheadlatentattention_pa_k_kernel(
         warm = keep.tile([P, 1], F32)
         nc.scalar.activation(out=warm[:], in_=cos_sin[:, 0, 0:1], func=ACT.Sqrt, bias=1.0, scale=0.0)
 
-        c_gain = keep.tile([P, Q_RANK], F32, tag="c_gain")
+        c_rows = keep.tile([P, Q_RANK], F32, tag="c_rows")
         square_sums = keep.tile([P, Q_RANK // BANK], F32)
         for blk in range(PLANES):
             banks = [psum.tile([P, BANK], F32, tag="sums", name="c_bank%d" % i) for i in range(4)]
             for g in range(DQ_PASSES):
-                w_block = block_pool.tile([P, DQ_BLOCK], I32, align_bytes=64, tag="w_block")
-                nc.sync.dma_start(
-                    out=w_block[:],
-                    in_=w_dq_words[g]
-                    .rearrange("p n t -> p (n t)")[:, 4 * DQ_BLOCK * blk : 4 * DQ_BLOCK * (blk + 1)]
-                    .bitcast(I32),
-                )
                 for i in range(4):
                     nc.tensor.matmul_mx(
                         out=banks[i][:],
                         lhsT=x_codes[:, g * P : (g + 1) * P].bitcast(FP8X4),
                         lhsT_scale=x_planes[:, g * P : (g + 1) * P],
-                        rhs=w_block[:, i * BANK : (i + 1) * BANK].bitcast(FP8X4),
+                        rhs=w_blocks[blk, g][:, i * BANK : (i + 1) * BANK].bitcast(FP8X4),
                         rhs_scale=dq_planes[4 * blk : P, g, i * BANK : (i + 1) * BANK],
                         start=(g == 0),
                         stop=(g == DQ_PASSES - 1),
@@ -201,9 +193,9 @@ def tile_multiheadlatentattention_pa_k_kernel(
                 c = 4 * blk + i
                 cols = slice(c * BANK, (c + 1) * BANK)
                 nc.scalar.activation(
-                    out=c_gain[:, cols], in_=banks[i][:], func=ACT.Square, accum_out=square_sums[:, c : c + 1]
+                    out=c_rows[:, cols], in_=banks[i][:], func=ACT.Square, accum_out=square_sums[:, c : c + 1]
                 )
-                nc.vector.tensor_tensor(out=c_gain[:, cols], in0=banks[i][:], in1=gain_all[:, cols], op=ALU.mult)
+                nc.vector.tensor_copy(out=c_rows[:, cols], in_=banks[i][:])
 
         square_sum = keep.tile([P, 1], F32)
         nc.vector.reduce_sum(out=square_sum[:], in_=square_sums[:], axis=mybir.AxisListType.X)
@@ -229,13 +221,24 @@ def tile_multiheadlatentattention_pa_k_kernel(
 
         for chunk in range(Q_RANK // H_CHUNK):
             h_rows = work.tile([P, H_CHUNK], BF16, tag="h_rows")
-            nc.vector.tensor_scalar(
-                out=h_rows[:],
-                in0=c_gain[:, chunk * H_CHUNK : (chunk + 1) * H_CHUNK],
-                scalar1=inv_rms[:, 0:1],
-                scalar2=None,
-                op0=ALU.mult,
-            )
+            for i in range(CHUNK_PASSES):
+                c = CHUNK_PASSES * chunk + i
+                spread = psum.tile([P, BANK], F32, tag="short", bufs=2)
+                nc.tensor.matmul(
+                    out=spread[:],
+                    lhsT=ident_bf[:, c : c + 1].to_broadcast([P, P]),
+                    rhs=gain_rows[:],
+                    start=True,
+                    stop=True,
+                )
+                nc.vector.scalar_tensor_tensor(
+                    out=h_rows[:, i * BANK : (i + 1) * BANK],
+                    in0=c_rows[:, c * BANK : (c + 1) * BANK],
+                    scalar=inv_rms[:, 0:1],
+                    in1=spread[:],
+                    op0=ALU.mult,
+                    op1=ALU.mult,
+                )
             cols = slice(chunk * H_CHUNK // 4, (chunk + 1) * H_CHUNK // 4)
             quantise_tokens(nc, psum, work, ident, h_rows[:], h_codes[:, cols], h_planes[:, cols])
             for g in range(chunk * CHUNK_PASSES, min((chunk + 1) * CHUNK_PASSES, MAIN_PASSES)):
@@ -255,7 +258,7 @@ def tile_multiheadlatentattention_pa_k_kernel(
                 .bitcast(I32),
             )
             w_tails.append(w_tail[:, bank % TAIL_BANKS, :, :])
-        q_rows = keep.tile([P, N_OUT + NOPE], F32, tag="c_gain")
+        q_rows = keep.tile([P, N_OUT + NOPE], F32, tag="c_rows")
         for bank in range(N_OUT // BANK):
             first_col = bank * BANK
             for j in range(TAIL_PASSES):

@@ -34,11 +34,13 @@ CHUNK_PASSES = H_CHUNK // K_PASS
 TAIL_PASSES = 2
 MAIN_PASSES = UQ_PASSES - TAIL_PASSES
 TAIL_BANKS = N_OUT // BANK // TAIL_PASSES
+GROUP = QK // ROPE
+BLOCKS = BANK // ROPE
 
 FLOPS = 2 * P * (D * Q_RANK + Q_RANK * N_OUT)
 
 
-def quantise_tokens(nc, psum, work, ident, rows, codes, planes):
+def group_tokens(nc, psum, work, ident, rows):
     words = rows.bitcast(F32)
     groups = words.shape[1] // (K_PASS // 2)
     grouped = work.tile([P, groups * K_PASS], BF16, align_bytes=64, tag="grouped")
@@ -55,7 +57,7 @@ def quantise_tokens(nc, psum, work, ident, rows, codes, planes):
             out=grouped_words[:, 2 * pair : 2 * pair + 2, :, :],
             in_=flipped[:].rearrange("p g u r -> p g r u"),
         )
-    nc.vector.quantize_mx(out=codes.bitcast(FP8X4), scales=planes, in_=grouped[:])
+    return grouped
 
 
 def tile_multiheadlatentattention_pa_k_kernel(
@@ -120,7 +122,8 @@ def tile_multiheadlatentattention_pa_k_kernel(
 
         x_codes = keep.tile([P, DQ_PASSES * P], U32, align_bytes=64)
         x_planes = keep.tile([P, DQ_PASSES * P], U8, align_bytes=64)
-        quantise_tokens(nc, psum, work, ident, x_rows[:], x_codes[:], x_planes[:])
+        x_grouped = group_tokens(nc, psum, work, ident, x_rows[:])
+        nc.vector.quantize_mx(out=x_codes[:].bitcast(FP8X4), scales=x_planes[:], in_=x_grouped[:])
 
         pos_int = keep.tile([P, 1], I32)
         for b in range(B):
@@ -219,71 +222,114 @@ def tile_multiheadlatentattention_pa_k_kernel(
                 stop=(g == UQ_PASSES - 1),
             )
 
-        for chunk in range(Q_RANK // H_CHUNK):
-            h_rows = work.tile([P, H_CHUNK], BF16, tag="h_rows")
-            for i in range(CHUNK_PASSES):
-                c = CHUNK_PASSES * chunk + i
-                spread = psum.tile([P, BANK], F32, tag="short", bufs=2)
-                nc.tensor.matmul(
-                    out=spread[:],
-                    lhsT=ident_bf[:, c : c + 1].to_broadcast([P, P]),
-                    rhs=gain_rows[:],
-                    start=True,
-                    stop=True,
-                )
-                nc.vector.scalar_tensor_tensor(
-                    out=h_rows[:, i * BANK : (i + 1) * BANK],
-                    in0=c_rows[:, c * BANK : (c + 1) * BANK],
-                    scalar=inv_rms[:, 0:1],
-                    in1=spread[:],
-                    op0=ALU.mult,
-                    op1=ALU.mult,
-                )
-            cols = slice(chunk * H_CHUNK // 4, (chunk + 1) * H_CHUNK // 4)
-            quantise_tokens(nc, psum, work, ident, h_rows[:], h_codes[:, cols], h_planes[:, cols])
-            for g in range(chunk * CHUNK_PASSES, min((chunk + 1) * CHUNK_PASSES, MAIN_PASSES)):
-                w_pass = pass_pool.tile([P, N_OUT], I32, align_bytes=64, tag="w_pass")
-                nc.sync.dma_start(out=w_pass[:], in_=w_uq_words[g].rearrange("p n t -> p (n t)").bitcast(I32))
-                for bank in range(N_OUT // BANK):
-                    uq_pass(g, bank, w_pass[:, bank * BANK : (bank + 1) * BANK])
+        h_chunks = {}
+        h_grouped = {}
 
-        w_tails = []
-        for bank in range(N_OUT // BANK):
-            if bank % TAIL_BANKS == 0:
-                w_tail = pass_pool.tile([P, TAIL_BANKS, TAIL_PASSES, BANK], I32, align_bytes=64, tag="w_pass")
-            nc.sync.dma_start(
-                out=w_tail[:, bank % TAIL_BANKS, :, :],
-                in_=w_uq_words[MAIN_PASSES:UQ_PASSES, :, bank * BANK : (bank + 1) * BANK, :]
-                .rearrange("g p n t -> p g (n t)")
-                .bitcast(I32),
+        def make_rows(g):
+            spread = psum.tile([P, BANK], F32, tag="short", bufs=2)
+            nc.tensor.matmul(
+                out=spread[:],
+                lhsT=ident_bf[:, g : g + 1].to_broadcast([P, P]),
+                rhs=gain_rows[:],
+                start=True,
+                stop=True,
             )
-            w_tails.append(w_tail[:, bank % TAIL_BANKS, :, :])
-        q_rows = keep.tile([P, N_OUT + NOPE], F32, tag="c_rows")
-        for bank in range(N_OUT // BANK):
+            chunk, i = divmod(g, CHUNK_PASSES)
+            if i == 0:
+                h_rows = work.tile([P, H_CHUNK], BF16, tag="h_rows", bufs=3)
+                h_chunks[chunk] = h_rows
+            nc.vector.scalar_tensor_tensor(
+                out=h_chunks[chunk][:, i * BANK : (i + 1) * BANK],
+                in0=c_rows[:, g * BANK : (g + 1) * BANK],
+                scalar=inv_rms[:, 0:1],
+                in1=spread[:],
+                op0=ALU.mult,
+                op1=ALU.mult,
+            )
+
+        def group(chunk):
+            h_grouped[chunk] = group_tokens(nc, psum, work, ident, h_chunks[chunk][:])
+
+        def quantise(chunk):
+            cols = slice(chunk * H_CHUNK // 4, (chunk + 1) * H_CHUNK // 4)
+            nc.vector.quantize_mx(
+                out=h_codes[:, cols].bitcast(FP8X4), scales=h_planes[:, cols], in_=h_grouped[chunk][:]
+            )
+
+        def main_pass(g):
+            w_pass = pass_pool.tile([P, N_OUT], I32, align_bytes=64, tag="w_pass")
+            nc.sync.dma_start(out=w_pass[:], in_=w_uq_words[g].rearrange("p n t -> p (n t)").bitcast(I32))
+            for bank in range(N_OUT // BANK):
+                uq_pass(g, bank, w_pass[:, bank * BANK : (bank + 1) * BANK])
+
+        with tc.manual_schedule(engines={mybir.EngineType.PE}):
+            make_rows(0)
+            make_rows(1)
+            group(0)
+            make_rows(2)
+            make_rows(3)
+            quantise(0)
+            for g in range(MAIN_PASSES):
+                chunk = g // CHUNK_PASSES
+                if g % CHUNK_PASSES == 0:
+                    group(chunk + 1)
+                main_pass(g)
+                if g % CHUNK_PASSES == 0:
+                    quantise(chunk + 1)
+                if g + 2 * CHUNK_PASSES < UQ_PASSES:
+                    make_rows(g + 2 * CHUNK_PASSES)
+
+        def rotated_blocks(bank):
+            return slice((GROUP - 1 - bank * BLOCKS) % GROUP, BLOCKS, GROUP)
+
+        def count(blocks):
+            return len(range(blocks.start, blocks.stop, blocks.step))
+
+        bank_order = sorted(range(N_OUT // BANK), key=lambda bank: -count(rotated_blocks(bank)))
+        w_tails = {}
+        for n, bank in enumerate(bank_order):
+            if n % TAIL_BANKS == 0:
+                w_tail = pass_pool.tile([P, TAIL_BANKS, TAIL_PASSES, BANK], I32, align_bytes=64, tag="w_pass")
+            step = 1 if bank == bank_order[-1] else TAIL_PASSES
+            for j in range(0, TAIL_PASSES, step):
+                nc.sync.dma_start(
+                    out=w_tail[:, n % TAIL_BANKS, j : j + step, :],
+                    in_=w_uq_words[MAIN_PASSES + j : MAIN_PASSES + j + step, :, bank * BANK : (bank + 1) * BANK, :]
+                    .rearrange("g p n t -> p g (n t)")
+                    .bitcast(I32),
+                )
+            w_tails[bank] = w_tail[:, n % TAIL_BANKS, :, :]
+        q_rows = keep.tile([P, N_OUT], F32, tag="c_rows")
+        for bank in bank_order:
             first_col = bank * BANK
             for j in range(TAIL_PASSES):
                 uq_pass(MAIN_PASSES + j, bank, w_tails[bank][:, j, :])
-            nc.scalar.copy(out=q_rows[:, first_col : first_col + BANK], in_=q_banks[bank][:])
-            heads = [h for h in range(H) if first_col <= h * QK + NOPE < first_col + BANK]
-            n_heads = len(heads)
-            rotated = q_rows[:, heads[0] * QK + NOPE : (heads[0] + n_heads) * QK + NOPE].rearrange(
-                "p (h f) -> p h f", f=QK
-            )[:, :, 0:ROPE]
+            sums = q_banks[bank][:].rearrange("p (b f) -> p b f", f=ROPE)
+            rows = q_rows[:, first_col : first_col + BANK].rearrange("p (b f) -> p b f", f=ROPE)
+            turned = rotated_blocks(bank)
+            n_heads = count(turned)
             products = work.tile([P, n_heads, 2, ROPE], F32, tag="products")
             nc.vector.tensor_tensor(
                 out=products[:],
-                in0=rotated.unsqueeze(2).to_broadcast([P, n_heads, 2, ROPE]),
+                in0=sums[:, turned, :].unsqueeze(2).to_broadcast([P, n_heads, 2, ROPE]),
                 in1=cos_sin[:].unsqueeze(1).to_broadcast([P, n_heads, 2, ROPE]),
                 op=ALU.mult,
             )
+            pairs = (turned.start + 1) % GROUP
+            rest = slice(0, 1) if pairs == GROUP - 1 else slice(pairs + 2 * GROUP, BLOCKS)
+            nc.scalar.copy(
+                out=rows[:, pairs : pairs + 2 * GROUP, :].rearrange("p (k b) f -> p k b f", b=GROUP)[:, :, 0:2, :],
+                in_=sums[:, pairs : pairs + 2 * GROUP, :].rearrange("p (k b) f -> p k b f", b=GROUP)[:, :, 0:2, :],
+            )
+            nc.scalar.copy(out=rows[:, rest, :], in_=sums[:, rest, :])
             nc.vector.tensor_tensor(
-                out=rotated[:, :, 0:HALF],
+                out=rows[:, turned, 0:HALF],
                 in0=products[:, :, 0, 0:HALF],
                 in1=products[:, :, 1, HALF:ROPE],
                 op=ALU.subtract,
             )
             nc.vector.tensor_tensor(
-                out=rotated[:, :, HALF:ROPE],
+                out=rows[:, turned, HALF:ROPE],
                 in0=products[:, :, 0, HALF:ROPE],
                 in1=products[:, :, 1, 0:HALF],
                 op=ALU.add,

import math
from contextlib import ExitStack

import concourse.mybir as mybir
from concourse.masks import make_identity

F32 = mybir.dt.float32
BF16 = mybir.dt.bfloat16
I32 = mybir.dt.int32
U32 = mybir.dt.uint32
U8 = mybir.dt.uint8
FP8X4 = mybir.dt.float8_e4m3fn_x4
ALU = mybir.AluOpType
ACT = mybir.ActivationFunctionType

B, S, D, H, NOPE, ROPE, Q_RANK = 2, 64, 1024, 16, 128, 64, 8192
HALF = ROPE // 2
DOUBLINGS = 5
assert 2**DOUBLINGS == HALF
QK = NOPE + ROPE
N_OUT = H * QK
EPS = 1e-6
THETA = 10000.0

P = 128
K_PASS = 512
BANK = 512
DQ_PASSES = D // K_PASS
UQ_PASSES = Q_RANK // K_PASS
PLANES = 4
DQ_BLOCK = Q_RANK // PLANES
H_CHUNK = 2 * K_PASS
CHUNK_PASSES = H_CHUNK // K_PASS
TAIL_PASSES = 2
MAIN_PASSES = UQ_PASSES - TAIL_PASSES
TAIL_BANKS = N_OUT // BANK // TAIL_PASSES
GROUP = QK // ROPE
BLOCKS = BANK // ROPE

FLOPS = 2 * P * (D * Q_RANK + Q_RANK * N_OUT)


def group_tokens(nc, psum, work, ident, rows):
    words = rows.bitcast(F32)
    groups = words.shape[1] // (K_PASS // 2)
    grouped = work.tile([P, groups * K_PASS], BF16, align_bytes=64, tag="grouped")
    grouped_words = grouped[:].bitcast(F32).rearrange("p (g r u) -> p g r u", r=P, u=2)
    for pair in range(groups // 2):
        flipped = psum.tile([P, 2, 2, P], F32, tag="short", bufs=2)
        for j in range(2):
            first = (2 * pair + j) * (K_PASS // 2)
            for u in range(2):
                nc.tensor.transpose(
                    flipped[:, j, u, :], words[:, first + u : first + K_PASS // 2 : 2], ident[:]
                )
        nc.scalar.copy(
            out=grouped_words[:, 2 * pair : 2 * pair + 2, :, :],
            in_=flipped[:].rearrange("p g u r -> p g r u"),
        )
    return grouped


def tile_multiheadlatentattention_pa_k_kernel(
    tc, x, w_dq_words, w_dq_scales, q_a_norm, w_uq_words, w_uq_scales, out
):
    nc = tc.nc
    out_flat = out.rearrange("b s h f -> (b s) (h f)")
    with ExitStack() as stack:
        keep = stack.enter_context(tc.tile_pool(name="keep", bufs=1))
        work = stack.enter_context(tc.tile_pool(name="work", bufs=2))
        block_pool = stack.enter_context(tc.tile_pool(name="block_words", bufs=8))
        pass_pool = stack.enter_context(tc.tile_pool(name="pass_words", bufs=7))
        psum = stack.enter_context(tc.psum_pool(name="psum", bufs=6))

        x_rows = keep.tile([P, D], BF16)
        nc.sync.dma_start(out=x_rows[:], in_=x.flatten_outer_dims())
        gain_rows = keep.tile([P, BANK], BF16)

        dq_planes = keep.tile([P, DQ_PASSES, DQ_BLOCK], U8, align_bytes=64)
        uq_planes = keep.tile([P, UQ_PASSES // PLANES, N_OUT], U8, align_bytes=64)
        nc.vector.memset(dq_planes[:].bitcast(I32), 0)
        nc.vector.memset(gain_rows[:], 0.0)
        nc.scalar.dma_start(
            out=gain_rows[0 : Q_RANK // BANK, :], in_=q_a_norm.rearrange("(c n) -> c n", n=BANK)
        )
        nc.vector.memset(uq_planes[:].bitcast(I32), 0)

        w_blocks = {}
        for blk in range(PLANES):
            for g in range(DQ_PASSES):
                w_block = block_pool.tile([P, DQ_BLOCK], I32, align_bytes=64, tag="w_block")
                nc.sync.dma_start(
                    out=w_block[:],
                    in_=w_dq_words[g]
                    .rearrange("p n t -> p (n t)")[:, 4 * DQ_BLOCK * blk : 4 * DQ_BLOCK * (blk + 1)]
                    .bitcast(I32),
                )
                w_blocks[blk, g] = w_block
                if blk == 0 and g == 0:
                    for gs in range(DQ_PASSES):
                        for quad in range(4):
                            nc.sync.dma_start(
                                out=dq_planes[32 * quad : 32 * quad + 16, gs, :].bitcast(I32),
                                in_=w_dq_scales[gs, 4 * quad : 4 * quad + 4, :]
                                .bitcast(I32)
                                .rearrange("r (j n) -> j r n", j=PLANES),
                            )
        for a in range(UQ_PASSES // PLANES):
            for quad in range(4):
                nc.sync.dma_start(
                    out=uq_planes[32 * quad : 32 * quad + 16, a, :].bitcast(I32),
                    in_=w_uq_scales[
                        PLANES * a : PLANES * (a + 1), 4 * quad : 4 * quad + 4, :
                    ].bitcast(I32),
                )


        ident = keep.tile([P, P], F32)
        make_identity(nc, ident[:])
        ident_bf = keep.tile([P, P], BF16)
        make_identity(nc, ident_bf[:])

        x_codes = keep.tile([P, DQ_PASSES * P], U32, align_bytes=64)
        x_planes = keep.tile([P, DQ_PASSES * P], U8, align_bytes=64)
        x_grouped = group_tokens(nc, psum, work, ident, x_rows[:])
        nc.vector.quantize_mx(out=x_codes[:].bitcast(FP8X4), scales=x_planes[:], in_=x_grouped[:])

        pos_int = keep.tile([P, 1], I32)
        for b in range(B):
            nc.gpsimd.iota(pos_int[b * S : (b + 1) * S, :], pattern=[[0, 1]], base=0, channel_multiplier=1)
        pos = keep.tile([P, 1], F32)
        nc.vector.tensor_copy(out=pos[:], in_=pos_int[:])
        base_turns = keep.tile([P, HALF], F32)
        nc.vector.tensor_scalar(
            out=base_turns[:, 0:1], in0=pos[:], scalar1=1.0 / (2.0 * math.pi), scalar2=None, op0=ALU.mult
        )
        for doubling in range(DOUBLINGS):
            width = 2**doubling
            nc.vector.tensor_scalar(
                out=base_turns[:, width : 2 * width],
                in0=base_turns[:, 0:width],
                scalar1=THETA ** (-width / HALF),
                scalar2=None,
                op0=ALU.mult,
            )
        turns = keep.tile([P, 2, 2, HALF], F32)
        for k, phase in enumerate((0.25, 0.0)):
            nc.vector.tensor_scalar(
                out=turns[:, k, :, :],
                in0=base_turns[:].unsqueeze(1).to_broadcast([P, 2, HALF]),
                scalar1=phase,
                scalar2=None,
                op0=ALU.add,
            )
        whole_int = keep.tile([P, 2, 2, HALF], I32)
        nc.vector.tensor_copy(out=whole_int[:], in_=turns[:])
        whole = keep.tile([P, 2, 2, HALF], F32)
        nc.vector.tensor_copy(out=whole[:], in_=whole_int[:])
        part = keep.tile([P, 2 * ROPE], F32)
        nc.vector.tensor_tensor(
            out=part[:],
            in0=turns[:].rearrange("p k j i -> p (k j i)"),
            in1=whole[:].rearrange("p k j i -> p (k j i)"),
            op=ALU.subtract,
        )
        minus_part = keep.tile([P, 2 * ROPE], F32)
        nc.vector.scalar_tensor_tensor(
            out=minus_part[:], in0=part[:], scalar=0.5, in1=part[:], op0=ALU.is_gt, op1=ALU.subtract
        )
        cos_sin = keep.tile([P, 2, ROPE], F32)
        nc.scalar.activation(
            out=cos_sin[:].rearrange("p k f -> p (k f)"),
            in_=minus_part[:],
            func=ACT.Sin,
            scale=-2.0 * math.pi,
        )
        warm = keep.tile([P, 1], F32)
        nc.scalar.activation(out=warm[:], in_=cos_sin[:, 0, 0:1], func=ACT.Sqrt, bias=1.0, scale=0.0)

        c_rows = keep.tile([P, Q_RANK], F32, tag="c_rows")
        square_sums = keep.tile([P, Q_RANK // BANK], F32)
        for blk in range(PLANES):
            banks = [psum.tile([P, BANK], F32, tag="sums", name="c_bank%d" % i) for i in range(4)]
            for g in range(DQ_PASSES):
                for i in range(4):
                    nc.tensor.matmul_mx(
                        out=banks[i][:],
                        lhsT=x_codes[:, g * P : (g + 1) * P].bitcast(FP8X4),
                        lhsT_scale=x_planes[:, g * P : (g + 1) * P],
                        rhs=w_blocks[blk, g][:, i * BANK : (i + 1) * BANK].bitcast(FP8X4),
                        rhs_scale=dq_planes[4 * blk : P, g, i * BANK : (i + 1) * BANK],
                        start=(g == 0),
                        stop=(g == DQ_PASSES - 1),
                    )
            for i in range(4):
                c = 4 * blk + i
                cols = slice(c * BANK, (c + 1) * BANK)
                nc.scalar.activation(
                    out=c_rows[:, cols], in_=banks[i][:], func=ACT.Square, accum_out=square_sums[:, c : c + 1]
                )
                nc.vector.tensor_copy(out=c_rows[:, cols], in_=banks[i][:])

        square_sum = keep.tile([P, 1], F32)
        nc.vector.reduce_sum(out=square_sum[:], in_=square_sums[:], axis=mybir.AxisListType.X)
        rms = keep.tile([P, 1], F32)
        nc.scalar.activation(out=rms[:], in_=square_sum[:], func=ACT.Sqrt, bias=EPS, scale=1.0 / Q_RANK)
        inv_rms = keep.tile([P, 1], F32)
        nc.vector.reciprocal(out=inv_rms[:], in_=rms[:])

        h_codes = keep.tile([P, UQ_PASSES * P], U32, align_bytes=64)
        h_planes = keep.tile([P, UQ_PASSES * P], U8, align_bytes=64)
        q_banks = [psum.tile([P, BANK], F32, tag="sums", name="q_bank%d" % i) for i in range(N_OUT // BANK)]

        def uq_pass(g, bank, words):
            nc.tensor.matmul_mx(
                out=q_banks[bank][:],
                lhsT=h_codes[:, g * P : (g + 1) * P].bitcast(FP8X4),
                lhsT_scale=h_planes[:, g * P : (g + 1) * P],
                rhs=words.bitcast(FP8X4),
                rhs_scale=uq_planes[4 * (g % PLANES) : P, g // PLANES, bank * BANK : (bank + 1) * BANK],
                start=(g == 0),
                stop=(g == UQ_PASSES - 1),
            )

        h_chunks = {}
        h_grouped = {}

        def make_rows(g):
            spread = psum.tile([P, BANK], F32, tag="short", bufs=2)
            nc.tensor.matmul(
                out=spread[:],
                lhsT=ident_bf[:, g : g + 1].to_broadcast([P, P]),
                rhs=gain_rows[:],
                start=True,
                stop=True,
            )
            chunk, i = divmod(g, CHUNK_PASSES)
            if i == 0:
                h_rows = work.tile([P, H_CHUNK], BF16, tag="h_rows", bufs=3)
                h_chunks[chunk] = h_rows
            nc.vector.scalar_tensor_tensor(
                out=h_chunks[chunk][:, i * BANK : (i + 1) * BANK],
                in0=c_rows[:, g * BANK : (g + 1) * BANK],
                scalar=inv_rms[:, 0:1],
                in1=spread[:],
                op0=ALU.mult,
                op1=ALU.mult,
            )

        def group(chunk):
            h_grouped[chunk] = group_tokens(nc, psum, work, ident, h_chunks[chunk][:])

        def quantise(chunk):
            cols = slice(chunk * H_CHUNK // 4, (chunk + 1) * H_CHUNK // 4)
            nc.vector.quantize_mx(
                out=h_codes[:, cols].bitcast(FP8X4), scales=h_planes[:, cols], in_=h_grouped[chunk][:]
            )

        def main_pass(g):
            w_pass = pass_pool.tile([P, N_OUT], I32, align_bytes=64, tag="w_pass")
            nc.sync.dma_start(out=w_pass[:], in_=w_uq_words[g].rearrange("p n t -> p (n t)").bitcast(I32))
            for bank in range(N_OUT // BANK):
                uq_pass(g, bank, w_pass[:, bank * BANK : (bank + 1) * BANK])

        with tc.manual_schedule(engines={mybir.EngineType.PE}):
            make_rows(0)
            make_rows(1)
            group(0)
            make_rows(2)
            make_rows(3)
            quantise(0)
            for g in range(MAIN_PASSES):
                chunk = g // CHUNK_PASSES
                if g % CHUNK_PASSES == 0:
                    group(chunk + 1)
                main_pass(g)
                if g % CHUNK_PASSES == 0:
                    quantise(chunk + 1)
                if g + 2 * CHUNK_PASSES < UQ_PASSES:
                    make_rows(g + 2 * CHUNK_PASSES)

        def rotated_blocks(bank):
            return slice((GROUP - 1 - bank * BLOCKS) % GROUP, BLOCKS, GROUP)

        def count(blocks):
            return len(range(blocks.start, blocks.stop, blocks.step))

        bank_order = sorted(range(N_OUT // BANK), key=lambda bank: -count(rotated_blocks(bank)))
        w_tails = {}
        for n, bank in enumerate(bank_order):
            if n % TAIL_BANKS == 0:
                w_tail = pass_pool.tile([P, TAIL_BANKS, TAIL_PASSES, BANK], I32, align_bytes=64, tag="w_pass")
            step = 1 if bank == bank_order[-1] else TAIL_PASSES
            for j in range(0, TAIL_PASSES, step):
                nc.sync.dma_start(
                    out=w_tail[:, n % TAIL_BANKS, j : j + step, :],
                    in_=w_uq_words[MAIN_PASSES + j : MAIN_PASSES + j + step, :, bank * BANK : (bank + 1) * BANK, :]
                    .rearrange("g p n t -> p g (n t)")
                    .bitcast(I32),
                )
            w_tails[bank] = w_tail[:, n % TAIL_BANKS, :, :]
        q_rows = keep.tile([P, N_OUT], F32, tag="c_rows")
        for bank in bank_order:
            first_col = bank * BANK
            for j in range(TAIL_PASSES):
                uq_pass(MAIN_PASSES + j, bank, w_tails[bank][:, j, :])
            sums = q_banks[bank][:].rearrange("p (b f) -> p b f", f=ROPE)
            rows = q_rows[:, first_col : first_col + BANK].rearrange("p (b f) -> p b f", f=ROPE)
            turned = rotated_blocks(bank)
            n_heads = count(turned)
            products = work.tile([P, n_heads, 2, ROPE], F32, tag="products")
            nc.vector.tensor_tensor(
                out=products[:],
                in0=sums[:, turned, :].unsqueeze(2).to_broadcast([P, n_heads, 2, ROPE]),
                in1=cos_sin[:].unsqueeze(1).to_broadcast([P, n_heads, 2, ROPE]),
                op=ALU.mult,
            )
            pairs = (turned.start + 1) % GROUP
            rest = slice(0, 1) if pairs == GROUP - 1 else slice(pairs + 2 * GROUP, BLOCKS)
            nc.scalar.copy(
                out=rows[:, pairs : pairs + 2 * GROUP, :].rearrange("p (k b) f -> p k b f", b=GROUP)[:, :, 0:2, :],
                in_=sums[:, pairs : pairs + 2 * GROUP, :].rearrange("p (k b) f -> p k b f", b=GROUP)[:, :, 0:2, :],
            )
            nc.scalar.copy(out=rows[:, rest, :], in_=sums[:, rest, :])
            nc.vector.tensor_tensor(
                out=rows[:, turned, 0:HALF],
                in0=products[:, :, 0, 0:HALF],
                in1=products[:, :, 1, HALF:ROPE],
                op=ALU.subtract,
            )
            nc.vector.tensor_tensor(
                out=rows[:, turned, HALF:ROPE],
                in0=products[:, :, 0, HALF:ROPE],
                in1=products[:, :, 1, 0:HALF],
                op=ALU.add,
            )
            nc.sync.dma_start(
                out=out_flat[:, first_col : first_col + BANK], in_=q_rows[:, first_col : first_col + BANK]
            )
